import numpy as np
import ml_dtypes


def mxq(x, axis, fmt="e4m3"):
    dtype, down = {"e4m3": (ml_dtypes.float8_e4m3fn, 7), "e5m2": (ml_dtypes.float8_e5m2, 14)}[fmt]
    v = np.moveaxis(np.asarray(x, np.float32).astype(ml_dtypes.bfloat16).astype(np.float64), axis, -1)
    blocks = v.reshape(v.shape[:-1] + (-1, 32))
    amax = np.abs(blocks).max(-1, keepdims=True)
    byte = np.maximum(np.where(amax > 0, np.frexp(amax)[1] - 1 + 127, 0) - down, 1)
    scale = np.exp2(byte - 127.0)
    codes = (blocks / scale).astype(np.float32).astype(dtype).astype(np.float64)
    return np.moveaxis((codes * scale).reshape(v.shape), -1, axis)


WIDE = False


def mx_kscale(k):
    if not WIDE:
        return np.ones(k)
    levels = np.array([10, -10, 5, -5, 0])
    a = np.random.permutation(np.resize(levels, k // 512 * 4)).reshape(k // 512, 4)
    idx = np.arange(k)
    return np.exp2(a[idx // 512, idx % 128 // 32])


BF16 = ml_dtypes.bfloat16


def bf(x):
    return np.asarray(x, np.float32).astype(BF16)


def f64(x):
    return np.asarray(x).astype(np.float64)


E2M1 = np.array([0.0, 0.5, 1.0, 1.5, 2.0, 3.0, 4.0, 6.0, -0.0, -0.5, -1.0, -1.5, -2.0, -3.0, -4.0, -6.0])


def pack_weight(w, fmt):
    k, n = w.shape
    w = f64(bf(w)).reshape(k // 32, 32, n)
    amax = np.abs(w).max(1)
    if fmt == "e4m3":
        byte = np.frexp(amax)[1] - 1 + 127 - 7
    else:
        mant, ex = np.frexp(amax / 6.0)
        byte = np.where(mant > 0.5, ex, ex - 1) + 127
    byte = np.clip(np.where(amax > 0, byte, 1), 1, 254)
    scaled = (w * np.exp2(127.0 - byte)[:, None, :]).reshape(k, n).astype(np.float32)
    by_word = np.ascontiguousarray(scaled.reshape(k // 512, 128, 4, n).transpose(0, 1, 3, 2))
    if fmt == "e4m3":
        words = by_word.astype(ml_dtypes.float8_e4m3fn).view(np.uint8)
    else:
        c = by_word.astype(ml_dtypes.float4_e2m1fn).view(np.uint8) & 0xF
        words = c[..., 0::2] | (c[..., 1::2] << 4)
    return np.ascontiguousarray(words), np.ascontiguousarray(byte.astype(np.uint8).reshape(k // 512, 16, n))


def unpack_weight(words, scales, fmt):
    g, p, n, _ = words.shape
    if fmt == "e4m3":
        vals = np.ascontiguousarray(words).view(ml_dtypes.float8_e4m3fn).astype(np.float64)
    else:
        nib = np.empty((g, p, n, 4), np.uint8)
        nib[..., 0::2] = words & 0xF
        nib[..., 1::2] = words >> 4
        vals = E2M1[nib]
    vals = vals * np.repeat(np.exp2(scales.astype(np.float64) - 127.0), 8, axis=1)[..., None]
    return vals.transpose(0, 1, 3, 2).reshape(g * 512, n)

def pack4(w):
    words, scales = pack_weight(w, "e2m1")
    return words.reshape(words.shape[0], 128, -1), scales


def unpack4(words, scales):
    return unpack_weight(words.reshape(words.shape[0], 128, -1, 2), scales, "e2m1")


B, K, N, G = 1024, 1024, 4096, 32


def erf(v):
    a = np.minimum(np.abs(v), 6.0)
    a2 = 2.0 * a * a
    term = a.copy()
    tot = a.copy()
    for n in range(1, 120):
        term *= a2
        term /= (2 * n + 1)
        tot += term
    return np.sign(v) * (2.0 / np.sqrt(np.pi)) * np.exp(-a * a) * tot


def setup_inputs():
    s = mx_kscale(K)
    x = bf(np.random.standard_normal((B, K)) * s)
    weight = np.random.standard_normal((N, K)) * 0.04 / s[None, :]
    weight_words, weight_scales = pack4(np.ascontiguousarray(weight.T))
    return {
        "x": x,
        "weight_words": weight_words,
        "weight_scales": weight_scales,
        "bias": bf(np.random.standard_normal(N) * 0.1),
        "bn_weight": bf(1.0 + 0.1 * np.random.standard_normal(N)),
        "bn_bias": bf(0.1 * np.random.standard_normal(N)),
        "gn_weight": bf(1.0 + 8.0 * np.random.standard_normal(N)),
        "gn_bias": bf(0.1 + 0.1 * np.random.standard_normal(N)),
        "num_groups": 32,
    }


def reference(x, weight_words, weight_scales, bias, bn_weight, bn_bias, gn_weight, gn_bias, num_groups):
    BN_EPS = 1e-5
    GN_EPS = 1e-5
    y = mxq(f64(x), 1, "e4m3") @ unpack4(weight_words, weight_scales)
    y = y + f64(bias)
    mean_bn = np.mean(y, axis=0, keepdims=True)
    var_bn = np.var(y, axis=0, keepdims=True)
    y = (y - mean_bn) * (1.0 / np.sqrt(var_bn + BN_EPS))
    y = y * f64(bn_weight) + f64(bn_bias)
    y = 0.5 * y * (1.0 + erf(y * (1.0 / np.sqrt(2.0))))
    Bn, C = y.shape
    Gn = int(num_groups)
    yg = y.reshape(Bn, Gn, C // Gn)
    mean_g = np.mean(yg, axis=2, keepdims=True)
    var_g = np.var(yg, axis=2, keepdims=True)
    yg = (yg - mean_g) * (1.0 / np.sqrt(var_g + GN_EPS))
    y = yg.reshape(Bn, C) * f64(gn_weight) + f64(gn_bias)
    y = np.mean(y, axis=1, keepdims=True)
    return np.maximum(y, 0.0)

@@ -1,0 +1,261 @@
+from contextlib import ExitStack
+
+import concourse.mybir as mybir
+from concourse.masks import make_identity
+
+F32 = mybir.dt.float32
+BF16 = mybir.dt.bfloat16
+U8 = mybir.dt.uint8
+U32 = mybir.dt.uint32
+I32 = mybir.dt.int32
+FP8X4 = mybir.dt.float8_e4m3fn_x4
+FP4X4 = mybir.dt.float4_e2m1fn_x4
+ACTF = mybir.ActivationFunctionType
+ALU = mybir.AluOpType
+AX = mybir.AxisListType
+
+P = 128
+B = 1024
+K = 1024
+N = 4096
+NG = 32
+NJ = B // P
+NPASS = K // 512
+EPS = 1e-5
+LO_DVE = 192
+
+FLOPS = 2 * B * K * N
+
+
+def tile_modelnew_kernel(
+    tc, x, weight_words, weight_scales, bias, bn_weight, bn_bias, gn_weight, gn_bias, num_groups, out
+):
+    nc = tc.nc
+    assert num_groups == NG
+    with ExitStack() as ctx:
+        keep = ctx.enter_context(tc.tile_pool(name="keep", bufs=1))
+        work = ctx.enter_context(tc.tile_pool(name="work", bufs=3))
+        small = ctx.enter_context(tc.tile_pool(name="small", bufs=4))
+        psy = ctx.enter_context(tc.psum_pool(name="psy", bufs=4))
+        pst = ctx.enter_context(tc.psum_pool(name="pst", bufs=3))
+        pss = ctx.enter_context(tc.psum_pool(name="pss", bufs=1))
+
+        ident = keep.tile([P, P], F32, name="ident")
+        make_identity(nc, ident[:])
+        ident_bf = keep.tile([P, P], BF16, name="ident_bf")
+        nc.vector.tensor_copy(out=ident_bf[:], in_=ident[:])
+        ones_bf = keep.tile([P, P], BF16, name="ones_bf")
+        nc.vector.memset(ones_bf[:], 1.0)
+        mhalf = keep.tile([P, 1], F32, name="mhalf")
+        nc.vector.memset(mhalf[:], -0.5)
+        zero1 = keep.tile([P, 1], F32, name="zero1")
+        nc.vector.memset(zero1[:], 0.0)
+        warm = keep.tile([P, 1], F32, name="warm")
+        nc.scalar.activation(out=warm[:], in_=zero1[:], func=ACTF.Gelu)
+
+        x_sb = keep.tile([P, NJ, K], BF16, name="x_sb")
+        x_v = x.rearrange("(p j) k -> p j k", j=NJ)
+        for jp in range(NJ // 2):
+            nc.sync.dma_start(out=x_sb[:, 2 * jp : 2 * jp + 2, :], in_=x_v[:, 2 * jp : 2 * jp + 2, :])
+
+        vin = keep.tile([P, P], BF16, name="vin")
+        for i, vec in enumerate((bn_weight, bn_bias, gn_weight, gn_bias)):
+            nc.scalar.dma_start(out=vin[32 * i : 32 * i + 32, :], in_=vec.rearrange("(g c) -> g c", c=P))
+
+        ws = keep.tile([P, NPASS, N], U8, name="ws", align_bytes=64)
+        nc.vector.memset(ws[:].bitcast(I32), 0)
+        for g in range(NPASS):
+            for bq in range(2):
+                for r in range(4):
+                    nc.sync.dma_start(
+                        out=ws[32 * bq + r : P : 64, g, :].bitcast(I32),
+                        in_=weight_scales[g, 4 * bq + r : 16 : 8, :].bitcast(I32),
+                    )
+        wq = keep.tile([P, NPASS, 2 * N], U8, name="wq", align_bytes=64)
+        for c in range(4):
+            for g in range(NPASS):
+                nc.sync.dma_start(
+                    out=wq[:, g, 2048 * c : 2048 * (c + 1)].bitcast(I32),
+                    in_=weight_words[g, :, 2048 * c : 2048 * (c + 1)].bitcast(I32),
+                )
+
+        vT = pst.tile([P, P], BF16, name="vT", tag="t")
+        nc.tensor.transpose(vT[:], vin[:], ident_bf[:])
+        bw2 = keep.tile([P, NG, 2], F32, name="bw2")
+        nc.vector.tensor_copy(out=bw2[:, :, 0], in_=vT[:, 0:32])
+        nc.vector.tensor_scalar(out=bw2[:, :, 1], in0=vT[:, 0:32], scalar1=-1.0, scalar2=None, op0=ALU.mult)
+        bnb = keep.tile([P, NG], F32, name="bnb")
+        nc.vector.tensor_copy(out=bnb[:], in_=vT[:, 32:64])
+        rw = keep.tile([P, NG, 2], BF16, name="rw")
+        nc.vector.memset(rw[:], 1.0)
+        nc.vector.tensor_copy(out=rw[:, :, 1], in_=vT[:, 64:96])
+        gwgb = keep.tile([P, 64], BF16, name="gwgb")
+        nc.vector.tensor_copy(out=gwgb[:], in_=vT[:, 64:128])
+        gsum_ps = pst.tile([P, 64], F32, name="gsum_ps", tag="t")
+        nc.tensor.matmul(gsum_ps[:], lhsT=ones_bf[:], rhs=gwgb[:], start=True, stop=True)
+        gsum = keep.tile([P, 64], F32, name="gsum")
+        nc.vector.tensor_copy(out=gsum[:], in_=gsum_ps[:])
+        gbt = keep.tile([P, 1], F32, name="gbt")
+        nc.vector.tensor_reduce(out=gbt[:], in_=gsum[:, 32:64], axis=AX.X, op=ALU.add)
+        gbs = keep.tile([P, 1], F32, name="gbs")
+        nc.vector.tensor_scalar(out=gbs[:], in0=gbt[:], scalar1=1.0 / N, scalar2=None, op0=ALU.mult)
+
+        x_w = x_sb[:].bitcast(F32)
+        grouped = keep.tile([P, NPASS, 4 * B], BF16, name="grouped", align_bytes=64)
+        grouped_w = grouped[:].bitcast(F32).rearrange("p g (c u) -> p g c u", u=2)
+        xq = keep.tile([P, NPASS, B], U32, name="xq", align_bytes=64)
+        xs = keep.tile([P, NPASS, B], U8, name="xs", align_bytes=64)
+        n_copy = 0
+        for jp in range(NJ // 2):
+            for g in range(NPASS):
+                xt = pst.tile([P, 2, 2, P], F32, name="xt", tag="t")
+                for u in range(2):
+                    for jj in range(2):
+                        nc.tensor.transpose(
+                            xt[:, u, jj, :],
+                            x_w[:, 2 * jp + jj, 256 * g + u : 256 * (g + 1) : 2],
+                            ident[:],
+                        )
+                dst = grouped_w[:, g, 256 * jp : 256 * (jp + 1), :]
+                src = xt[:].rearrange("p u j c -> p (j c) u")
+                if n_copy % 2 == 0:
+                    nc.vector.tensor_copy(out=dst, in_=src)
+                else:
+                    nc.scalar.copy(out=dst, in_=src)
+                n_copy += 1
+            if jp % 2 == 1:
+                hf = jp // 2
+                for g in range(NPASS):
+                    nc.vector.quantize_mx(
+                        out=xq[:, g, 512 * hf : 512 * (hf + 1)].bitcast(FP8X4),
+                        scales=xs[:, g, 512 * hf : 512 * (hf + 1)],
+                        in_=grouped[:, g, 2048 * hf : 2048 * (hf + 1)],
+                    )
+
+        s_ps = pss.tile([P, NJ, NG, 2], F32, name="s_ps")
+        s2 = keep.tile([P, NJ, NG], F32, name="s2")
+        ys = {}
+        coef = {}
+        acts = {}
+
+        def stage_mx(G):
+            y = []
+            for hf in range(2):
+                y.append(psy.tile([P, 512], F32, name="y%d" % hf, tag="y"))
+            for hf in range(2):
+                for g in range(NPASS):
+                    nc.tensor.matmul_mx(
+                        out=y[hf][:],
+                        lhsT=wq[:, g, 256 * G : 256 * (G + 1)].bitcast(FP4X4),
+                        lhsT_scale=ws[:, g, P * G : P * (G + 1)],
+                        rhs=xq[:, g, 512 * hf : 512 * (hf + 1)].bitcast(FP8X4),
+                        rhs_scale=xs[:, g, 512 * hf : 512 * (hf + 1)],
+                        start=(g == 0),
+                        stop=(g == NPASS - 1),
+                    )
+            ys[G] = y
+
+        def stage_stats(G):
+            y = ys[G]
+            st = small.tile([P, 2, 6], F32, name="st")
+            for hf in range(2):
+                nc.vector.bn_stats(out=st[:, hf, :], in_=y[hf][:])
+            mv = small.tile([P, 2], F32, name="mv")
+            nc.vector.bn_aggr(out=mv[:], in_=st[:].rearrange("p a b -> p (a b)"))
+            ve = small.tile([P, 1], F32, name="ve")
+            nc.vector.tensor_scalar(out=ve[:], in0=mv[:, 1:2], scalar1=EPS, scalar2=None, op0=ALU.add)
+            mb = small.tile([P, 1], F32, name="mb")
+            nc.vector.tensor_tensor(out=mb[:], in0=mv[:, 0:1], in1=bw2[:, G, 1:2], op=ALU.mult)
+            rstd = small.tile([P, 1], F32, name="rstd")
+            nc.gpsimd.tensor_tensor(out=rstd[:], in0=ve[:], in1=mhalf[:], op=ALU.pow)
+            aa = small.tile([P, 1], F32, name="aa")
+            nc.gpsimd.tensor_tensor(out=aa[:], in0=rstd[:], in1=bw2[:, G, 0:1], op=ALU.mult)
+            cc = small.tile([P, 1], F32, name="cc")
+            nc.gpsimd.tensor_scalar(
+                out=cc[:], in0=mb[:], scalar1=rstd[:, 0:1], scalar2=bnb[:, G : G + 1], op0=ALU.mult, op1=ALU.add
+            )
+            coef[G] = (aa, cc)
+
+        def stage_gelu(G):
+            y = ys[G]
+            aa, cc = coef[G]
+            g32 = work.tile([P, B], F32, name="g32")
+            hi = work.tile([P, B], BF16, name="hi")
+            lo = work.tile([P, B], BF16, name="lo")
+            for hf in range(2):
+                cols = slice(512 * hf, 512 * (hf + 1))
+                nc.scalar.activation(
+                    out=g32[:, cols], in_=y[hf][:], func=ACTF.Gelu, bias=cc[:, 0:1], scale=aa[:, 0:1]
+                )
+            acts[G] = (g32, hi, lo)
+
+        def stage_split(G, hf):
+            g32, hi, lo = acts[G]
+            c0 = 512 * hf
+            nc.vector.tensor_copy(out=hi[:, c0 : c0 + 512], in_=g32[:, c0 : c0 + 512])
+            cd = slice(c0, c0 + LO_DVE)
+            nc.vector.tensor_tensor(out=lo[:, cd], in0=g32[:, cd], in1=hi[:, cd], op=ALU.subtract)
+            cp = slice(c0 + LO_DVE, c0 + 512)
+            nc.gpsimd.tensor_tensor(out=lo[:, cp], in0=g32[:, cp], in1=hi[:, cp], op=ALU.subtract)
+
+        def stage_transpose(G, hf):
+            g32 = acts[G][0]
+            gT = pst.tile([P, 4, P], F32, name="gT", tag="t")
+            for q in range(4):
+                j = 4 * hf + q
+                nc.tensor.transpose(gT[:, q, :], g32[:, P * j : P * (j + 1)], ident[:])
+            for q in range(4):
+                j = 4 * hf + q
+                junk = small.tile([P, P], BF16, name="junk")
+                nc.scalar.activation(out=junk[:], in_=gT[:, q, :], func=ACTF.Square, accum_out=s2[:, j, G : G + 1])
+
+        def stage_sums(G):
+            g32, hi, lo = acts[G]
+            for j in range(NJ):
+                nc.tensor.matmul(
+                    s_ps[:, j, G, :], lhsT=hi[:, P * j : P * (j + 1)], rhs=rw[:, G, :], start=True, stop=False
+                )
+                nc.tensor.matmul(
+                    s_ps[:, j, G, :], lhsT=lo[:, P * j : P * (j + 1)], rhs=rw[:, G, :], start=False, stop=True
+                )
+
+        for T in range(NG + 2):
+            if T < NG:
+                stage_mx(T)
+                stage_stats(T)
+            if 1 <= T <= NG:
+                stage_gelu(T - 1)
+                stage_transpose(T - 1, 0)
+                stage_split(T - 1, 0)
+            if 2 <= T:
+                stage_sums(T - 2)
+            if 1 <= T <= NG:
+                stage_transpose(T - 1, 1)
+                stage_split(T - 1, 1)
+
+        shp = [P, NJ, NG]
+        mean = keep.tile(shp, F32, name="mean")
+        nc.vector.tensor_scalar(out=mean[:], in0=s_ps[:, :, :, 0], scalar1=1.0 / P, scalar2=None, op0=ALU.mult)
+        msq = keep.tile(shp, F32, name="msq")
+        nc.vector.tensor_tensor(out=msq[:], in0=mean[:], in1=mean[:], op=ALU.mult)
+        var = keep.tile(shp, F32, name="var")
+        nc.vector.scalar_tensor_tensor(
+            out=var[:], in0=s2[:], scalar=1.0 / P, in1=msq[:], op0=ALU.mult, op1=ALU.subtract
+        )
+        nc.vector.tensor_scalar(out=var[:], in0=var[:], scalar1=0.0, scalar2=EPS, op0=ALU.max, op1=ALU.add)
+        sd = keep.tile(shp, F32, name="sd")
+        nc.scalar.activation(out=sd[:], in_=var[:], func=ACTF.Sqrt)
+        rinv = keep.tile(shp, F32, name="rinv")
+        nc.vector.reciprocal(out=rinv[:], in_=sd[:])
+        mg = keep.tile(shp, F32, name="mg")
+        nc.vector.tensor_tensor(
+            out=mg[:], in0=mean[:], in1=gsum[:, 0:32].unsqueeze(1).to_broadcast(shp), op=ALU.mult
+        )
+        num = keep.tile(shp, F32, name="num")
+        nc.vector.tensor_tensor(out=num[:], in0=s_ps[:, :, :, 1], in1=mg[:], op=ALU.subtract)
+        nc.vector.tensor_tensor(out=num[:], in0=num[:], in1=rinv[:], op=ALU.mult)
+        tot = keep.tile([P, NJ], F32, name="tot")
+        nc.vector.tensor_reduce(out=tot[:], in_=num[:], axis=AX.X, op=ALU.add)
+        res = keep.tile([P, NJ], F32, name="res")
+        nc.scalar.activation(out=res[:], in_=tot[:], func=ACTF.Relu, bias=gbs[:, 0:1], scale=1.0 / N)
+        nc.sync.dma_start(out=out.rearrange("(p j) o -> p (j o)", j=NJ), in_=res[:])

@@ -22,7 +22,7 @@ NG = 32
 NJ = B // P
 NPASS = K // 512
 EPS = 1e-5
-LO_DVE = 192
+LO_DVE = 288
 
 FLOPS = 2 * B * K * N
 
@@ -34,10 +34,10 @@ def tile_modelnew_kernel(
     assert num_groups == NG
     with ExitStack() as ctx:
         keep = ctx.enter_context(tc.tile_pool(name="keep", bufs=1))
-        work = ctx.enter_context(tc.tile_pool(name="work", bufs=3))
-        small = ctx.enter_context(tc.tile_pool(name="small", bufs=4))
-        psy = ctx.enter_context(tc.psum_pool(name="psy", bufs=4))
-        pst = ctx.enter_context(tc.psum_pool(name="pst", bufs=3))
+        work = ctx.enter_context(tc.tile_pool(name="work", bufs=5))
+        small = ctx.enter_context(tc.tile_pool(name="small", bufs=6))
+        psy = ctx.enter_context(tc.psum_pool(name="psy", bufs=5))
+        pst = ctx.enter_context(tc.psum_pool(name="pst", bufs=2))
         pss = ctx.enter_context(tc.psum_pool(name="pss", bufs=1))
 
         ident = keep.tile([P, P], F32, name="ident")
@@ -108,7 +108,7 @@ def tile_modelnew_kernel(
         n_copy = 0
         for jp in range(NJ // 2):
             for g in range(NPASS):
-                xt = pst.tile([P, 2, 2, P], F32, name="xt", tag="t")
+                xt = psy.tile([P, 2, 2, P], F32, name="xt", tag="y")
                 for u in range(2):
                     for jj in range(2):
                         nc.tensor.transpose(
@@ -137,6 +137,8 @@ def tile_modelnew_kernel(
         ys = {}
         coef = {}
         acts = {}
+        stats = {}
+        gts = {}
 
         def stage_mx(G):
             y = []
@@ -160,12 +162,23 @@ def tile_modelnew_kernel(
             st = small.tile([P, 2, 6], F32, name="st")
             for hf in range(2):
                 nc.vector.bn_stats(out=st[:, hf, :], in_=y[hf][:])
+            stats[G] = st
+
+        def stage_aggr(G):
             mv = small.tile([P, 2], F32, name="mv")
-            nc.vector.bn_aggr(out=mv[:], in_=st[:].rearrange("p a b -> p (a b)"))
+            nc.vector.bn_aggr(out=mv[:], in_=stats[G][:].rearrange("p a b -> p (a b)"))
+            stats[G] = mv
+
+        def stage_eps(G):
+            mv = stats[G]
             ve = small.tile([P, 1], F32, name="ve")
             nc.vector.tensor_scalar(out=ve[:], in0=mv[:, 1:2], scalar1=EPS, scalar2=None, op0=ALU.add)
             mb = small.tile([P, 1], F32, name="mb")
             nc.vector.tensor_tensor(out=mb[:], in0=mv[:, 0:1], in1=bw2[:, G, 1:2], op=ALU.mult)
+            stats[G] = (ve, mb)
+
+        def stage_chain(G):
+            ve, mb = stats[G]
             rstd = small.tile([P, 1], F32, name="rstd")
             nc.gpsimd.tensor_tensor(out=rstd[:], in0=ve[:], in1=mhalf[:], op=ALU.pow)
             aa = small.tile([P, 1], F32, name="aa")
@@ -189,21 +202,34 @@ def tile_modelnew_kernel(
                 )
             acts[G] = (g32, hi, lo)
 
-        def stage_split(G, hf):
+        def stage_hi(G, hf):
             g32, hi, lo = acts[G]
             c0 = 512 * hf
             nc.vector.tensor_copy(out=hi[:, c0 : c0 + 512], in_=g32[:, c0 : c0 + 512])
-            cd = slice(c0, c0 + LO_DVE)
+
+        def stage_lo_dve(G, hf):
+            g32, hi, lo = acts[G]
+            cd = slice(512 * hf, 512 * hf + LO_DVE)
             nc.vector.tensor_tensor(out=lo[:, cd], in0=g32[:, cd], in1=hi[:, cd], op=ALU.subtract)
-            cp = slice(c0 + LO_DVE, c0 + 512)
+
+        def stage_lo_pool(G, hf):
+            g32, hi, lo = acts[G]
+            cp = slice(512 * hf + LO_DVE, 512 * hf + 512)
             nc.gpsimd.tensor_tensor(out=lo[:, cp], in0=g32[:, cp], in1=hi[:, cp], op=ALU.subtract)
 
-        def stage_transpose(G, hf):
+        def stage_transpose(G):
             g32 = acts[G][0]
-            gT = pst.tile([P, 4, P], F32, name="gT", tag="t")
-            for q in range(4):
-                j = 4 * hf + q
-                nc.tensor.transpose(gT[:, q, :], g32[:, P * j : P * (j + 1)], ident[:])
+            tiles = []
+            for hf in range(2):
+                gT = pst.tile([P, 4, P], F32, name="gT", tag="t")
+                for q in range(4):
+                    j = 4 * hf + q
+                    nc.tensor.transpose(gT[:, q, :], g32[:, P * j : P * (j + 1)], ident[:])
+                tiles.append(gT)
+            gts[G] = tiles
+
+        def stage_square(G, hf):
+            gT = gts[G][hf]
             for q in range(4):
                 j = 4 * hf + q
                 junk = small.tile([P, P], BF16, name="junk")
@@ -219,19 +245,36 @@ def tile_modelnew_kernel(
                     s_ps[:, j, G, :], lhsT=lo[:, P * j : P * (j + 1)], rhs=rw[:, G, :], start=False, stop=True
                 )
 
-        for T in range(NG + 2):
-            if T < NG:
-                stage_mx(T)
-                stage_stats(T)
-            if 1 <= T <= NG:
-                stage_gelu(T - 1)
-                stage_transpose(T - 1, 0)
-                stage_split(T - 1, 0)
-            if 2 <= T:
-                stage_sums(T - 2)
-            if 1 <= T <= NG:
-                stage_transpose(T - 1, 1)
-                stage_split(T - 1, 1)
+        def live(G):
+            return 0 <= G < NG
+
+        with tc.manual_schedule():
+            for T in range(NG + 3):
+                if live(T - 2):
+                    stage_hi(T - 2, 1)
+                    stage_lo_dve(T - 2, 1)
+                    stage_lo_pool(T - 2, 0)
+                    stage_lo_pool(T - 2, 1)
+                if live(T - 3):
+                    stage_square(T - 3, 1)
+                if live(T):
+                    stage_mx(T)
+                    stage_stats(T)
+                if live(T - 1):
+                    stage_gelu(T - 1)
+                    stage_hi(T - 1, 0)
+                if live(T):
+                    stage_aggr(T)
+                if live(T - 1):
+                    stage_lo_dve(T - 1, 0)
+                if live(T):
+                    stage_eps(T)
+                    stage_chain(T)
+                if live(T - 2):
+                    stage_transpose(T - 2)
+                    stage_square(T - 2, 0)
+                if live(T - 3):
+                    stage_sums(T - 3)
 
         shp = [P, NJ, NG]
         mean = keep.tile(shp, F32, name="mean")

@@ -22,7 +22,8 @@ NG = 32
 NJ = B // P
 NPASS = K // 512
 EPS = 1e-5
-LO_DVE = 288
+NW = 32
+KSPLIT = 3
 
 FLOPS = 2 * B * K * N
 
@@ -37,7 +38,7 @@ def tile_modelnew_kernel(
         work = ctx.enter_context(tc.tile_pool(name="work", bufs=5))
         small = ctx.enter_context(tc.tile_pool(name="small", bufs=6))
         psy = ctx.enter_context(tc.psum_pool(name="psy", bufs=5))
-        pst = ctx.enter_context(tc.psum_pool(name="pst", bufs=2))
+        pst = ctx.enter_context(tc.psum_pool(name="pst", bufs=1))
         pss = ctx.enter_context(tc.psum_pool(name="pss", bufs=1))
 
         ident = keep.tile([P, P], F32, name="ident")
@@ -79,19 +80,22 @@ def tile_modelnew_kernel(
                     in_=weight_words[g, :, 2048 * c : 2048 * (c + 1)].bitcast(I32),
                 )
 
-        vT = pst.tile([P, P], BF16, name="vT", tag="t")
+        vT = pst.tile([P, P], BF16, name="vT", tag="gT0")
         nc.tensor.transpose(vT[:], vin[:], ident_bf[:])
         bw2 = keep.tile([P, NG, 2], F32, name="bw2")
         nc.vector.tensor_copy(out=bw2[:, :, 0], in_=vT[:, 0:32])
         nc.vector.tensor_scalar(out=bw2[:, :, 1], in0=vT[:, 0:32], scalar1=-1.0, scalar2=None, op0=ALU.mult)
         bnb = keep.tile([P, NG], F32, name="bnb")
         nc.vector.tensor_copy(out=bnb[:], in_=vT[:, 32:64])
-        rw = keep.tile([P, NG, 2], BF16, name="rw")
-        nc.vector.memset(rw[:], 1.0)
+        rw = keep.tile([P, NG, NW], BF16, name="rw")
+        nc.vector.memset(rw[:], 0.0)
+        nc.vector.memset(rw[:, :, 0], 1.0)
         nc.vector.tensor_copy(out=rw[:, :, 1], in_=vT[:, 64:96])
+        rw32 = keep.tile([P, NG, NW], F32, name="rw32")
+        nc.vector.tensor_copy(out=rw32[:], in_=rw[:])
         gwgb = keep.tile([P, 64], BF16, name="gwgb")
         nc.vector.tensor_copy(out=gwgb[:], in_=vT[:, 64:128])
-        gsum_ps = pst.tile([P, 64], F32, name="gsum_ps", tag="t")
+        gsum_ps = pst.tile([P, 64], F32, name="gsum_ps", tag="gT1")
         nc.tensor.matmul(gsum_ps[:], lhsT=ones_bf[:], rhs=gwgb[:], start=True, stop=True)
         gsum = keep.tile([P, 64], F32, name="gsum")
         nc.vector.tensor_copy(out=gsum[:], in_=gsum_ps[:])
@@ -132,8 +136,10 @@ def tile_modelnew_kernel(
                         in_=grouped[:, g, 2048 * hf : 2048 * (hf + 1)],
                     )
 
-        s_ps = pss.tile([P, NJ, NG, 2], F32, name="s_ps")
-        s2 = keep.tile([P, NJ, NG], F32, name="s2")
+        s_ps = pss.tile([P, NG, NJ, 2], F32, name="s_ps")
+        s_flat = s_ps[:].rearrange("p g j c -> p (g j c)")
+        s2 = keep.tile([P, NG, 4], F32, name="s2")
+        st2 = keep.tile([P, NG, 4, 6], F32, name="st2")
         ys = {}
         coef = {}
         acts = {}
@@ -175,115 +181,118 @@ def tile_modelnew_kernel(
             nc.vector.tensor_scalar(out=ve[:], in0=mv[:, 1:2], scalar1=EPS, scalar2=None, op0=ALU.add)
             mb = small.tile([P, 1], F32, name="mb")
             nc.vector.tensor_tensor(out=mb[:], in0=mv[:, 0:1], in1=bw2[:, G, 1:2], op=ALU.mult)
-            stats[G] = (ve, mb)
-
-        def stage_chain(G):
-            ve, mb = stats[G]
             rstd = small.tile([P, 1], F32, name="rstd")
             nc.gpsimd.tensor_tensor(out=rstd[:], in0=ve[:], in1=mhalf[:], op=ALU.pow)
-            aa = small.tile([P, 1], F32, name="aa")
-            nc.gpsimd.tensor_tensor(out=aa[:], in0=rstd[:], in1=bw2[:, G, 0:1], op=ALU.mult)
-            cc = small.tile([P, 1], F32, name="cc")
-            nc.gpsimd.tensor_scalar(
-                out=cc[:], in0=mb[:], scalar1=rstd[:, 0:1], scalar2=bnb[:, G : G + 1], op0=ALU.mult, op1=ALU.add
-            )
-            coef[G] = (aa, cc)
+            stats[G] = (rstd, mb)
 
         def stage_gelu(G):
             y = ys[G]
-            aa, cc = coef[G]
+            rstd, mb = stats[G]
+            aa = small.tile([P, 1], F32, name="aa")
+            nc.scalar.activation(out=aa[:], in_=bw2[:, G, 0:1], func=ACTF.Copy, scale=rstd[:, 0:1])
+            cc = small.tile([P, 1], F32, name="cc")
+            nc.scalar.activation(
+                out=cc[:], in_=mb[:], func=ACTF.Identity, bias=bnb[:, G : G + 1], scale=rstd[:, 0:1]
+            )
             g32 = work.tile([P, B], F32, name="g32")
-            hi = work.tile([P, B], BF16, name="hi")
-            lo = work.tile([P, B], BF16, name="lo")
             for hf in range(2):
                 cols = slice(512 * hf, 512 * (hf + 1))
                 nc.scalar.activation(
                     out=g32[:, cols], in_=y[hf][:], func=ACTF.Gelu, bias=cc[:, 0:1], scale=aa[:, 0:1]
                 )
-            acts[G] = (g32, hi, lo)
+            acts[G] = g32
 
-        def stage_hi(G, hf):
-            g32, hi, lo = acts[G]
-            c0 = 512 * hf
-            nc.vector.tensor_copy(out=hi[:, c0 : c0 + 512], in_=g32[:, c0 : c0 + 512])
+        def stage_hi(G):
+            hi = work.tile([P, P * KSPLIT], BF16, name="hi")
+            nc.vector.tensor_copy(out=hi[:], in_=acts[G][:, 0 : P * KSPLIT])
+            coef[G] = hi
 
-        def stage_lo_dve(G, hf):
-            g32, hi, lo = acts[G]
-            cd = slice(512 * hf, 512 * hf + LO_DVE)
-            nc.vector.tensor_tensor(out=lo[:, cd], in0=g32[:, cd], in1=hi[:, cd], op=ALU.subtract)
-
-        def stage_lo_pool(G, hf):
-            g32, hi, lo = acts[G]
-            cp = slice(512 * hf + LO_DVE, 512 * hf + 512)
-            nc.gpsimd.tensor_tensor(out=lo[:, cp], in0=g32[:, cp], in1=hi[:, cp], op=ALU.subtract)
+        def stage_lo(G):
+            hi = coef[G]
+            lo = work.tile([P, P * KSPLIT], BF16, name="lo")
+            nc.vector.tensor_tensor(out=lo[:], in0=acts[G][:, 0 : P * KSPLIT], in1=hi[:], op=ALU.subtract)
+            coef[G] = (hi, lo)
 
         def stage_transpose(G):
-            g32 = acts[G][0]
+            g32 = acts[G]
             tiles = []
             for hf in range(2):
-                gT = pst.tile([P, 4, P], F32, name="gT", tag="t")
+                gT = pst.tile([P, 4, P], F32, name="gT%d" % hf)
                 for q in range(4):
                     j = 4 * hf + q
                     nc.tensor.transpose(gT[:, q, :], g32[:, P * j : P * (j + 1)], ident[:])
                 tiles.append(gT)
             gts[G] = tiles
 
-        def stage_square(G, hf):
-            gT = gts[G][hf]
+        def stage_square_act(G):
+            gT = gts[G][0]
             for q in range(4):
-                j = 4 * hf + q
                 junk = small.tile([P, P], BF16, name="junk")
-                nc.scalar.activation(out=junk[:], in_=gT[:, q, :], func=ACTF.Square, accum_out=s2[:, j, G : G + 1])
+                nc.scalar.activation(out=junk[:], in_=gT[:, q, :], func=ACTF.Square, accum_out=s2[:, G, q : q + 1])
+
+        def stage_square_dve(G):
+            gT = gts[G][1]
+            for q in range(4):
+                nc.vector.bn_stats(out=st2[:, G, q, :], in_=gT[:, q, :])
 
         def stage_sums(G):
-            g32, hi, lo = acts[G]
+            g32 = acts[G]
+            hi, lo = coef[G]
             for j in range(NJ):
-                nc.tensor.matmul(
-                    s_ps[:, j, G, :], lhsT=hi[:, P * j : P * (j + 1)], rhs=rw[:, G, :], start=True, stop=False
-                )
-                nc.tensor.matmul(
-                    s_ps[:, j, G, :], lhsT=lo[:, P * j : P * (j + 1)], rhs=rw[:, G, :], start=False, stop=True
-                )
+                cols = slice(P * j, P * (j + 1))
+                first = 2 * (NJ * G + j)
+                width = min(NW, 512 - first)
+                dst = s_flat[:, first : first + width]
+                if j < KSPLIT:
+                    nc.tensor.matmul(dst, lhsT=hi[:, cols], rhs=rw[:, G, 0:width], start=True, stop=False)
+                    nc.tensor.matmul(dst, lhsT=lo[:, cols], rhs=rw[:, G, 0:width], start=False, stop=True)
+                else:
+                    nc.tensor.matmul(dst, lhsT=g32[:, cols], rhs=rw32[:, G, 0:width], start=True, stop=True)
 
         def live(G):
             return 0 <= G < NG
 
         with tc.manual_schedule():
             for T in range(NG + 3):
-                if live(T - 2):
-                    stage_hi(T - 2, 1)
-                    stage_lo_dve(T - 2, 1)
-                    stage_lo_pool(T - 2, 0)
-                    stage_lo_pool(T - 2, 1)
                 if live(T - 3):
-                    stage_square(T - 3, 1)
+                    stage_square_dve(T - 3)
+                    stage_square_act(T - 3)
                 if live(T):
                     stage_mx(T)
                     stage_stats(T)
-                if live(T - 1):
-                    stage_gelu(T - 1)
-                    stage_hi(T - 1, 0)
+                if live(T - 2):
+                    stage_hi(T - 2)
                 if live(T):
                     stage_aggr(T)
-                if live(T - 1):
-                    stage_lo_dve(T - 1, 0)
+                if live(T - 2):
+                    stage_lo(T - 2)
                 if live(T):
                     stage_eps(T)
-                    stage_chain(T)
+                if live(T - 1):
+                    stage_gelu(T - 1)
                 if live(T - 2):
                     stage_transpose(T - 2)
-                    stage_square(T - 2, 0)
                 if live(T - 3):
                     stage_sums(T - 3)
 
-        shp = [P, NJ, NG]
+        shp = [P, NG, NJ]
+        half = [P, NG, 4]
         mean = keep.tile(shp, F32, name="mean")
         nc.vector.tensor_scalar(out=mean[:], in0=s_ps[:, :, :, 0], scalar1=1.0 / P, scalar2=None, op0=ALU.mult)
-        msq = keep.tile(shp, F32, name="msq")
-        nc.vector.tensor_tensor(out=msq[:], in0=mean[:], in1=mean[:], op=ALU.mult)
         var = keep.tile(shp, F32, name="var")
+        dd = keep.tile(half, F32, name="dd")
+        nc.vector.tensor_tensor(out=dd[:], in0=st2[:, :, :, 1], in1=st2[:, :, :, 4], op=ALU.subtract)
+        dq = keep.tile(half, F32, name="dq")
+        nc.vector.scalar_tensor_tensor(out=dq[:], in0=dd[:], scalar=0.25, in1=dd[:], op0=ALU.mult, op1=ALU.mult)
+        m2 = keep.tile(half, F32, name="m2")
+        nc.vector.tensor_tensor(out=m2[:], in0=st2[:, :, :, 2], in1=st2[:, :, :, 5], op=ALU.add)
         nc.vector.scalar_tensor_tensor(
-            out=var[:], in0=s2[:], scalar=1.0 / P, in1=msq[:], op0=ALU.mult, op1=ALU.subtract
+            out=var[:, :, 4:8], in0=m2[:], scalar=1.0 / P, in1=dq[:], op0=ALU.mult, op1=ALU.add
+        )
+        msq = keep.tile(half, F32, name="msq")
+        nc.vector.tensor_tensor(out=msq[:], in0=mean[:, :, 0:4], in1=mean[:, :, 0:4], op=ALU.mult)
+        nc.vector.scalar_tensor_tensor(
+            out=var[:, :, 0:4], in0=s2[:], scalar=1.0 / P, in1=msq[:], op0=ALU.mult, op1=ALU.subtract
         )
         nc.vector.tensor_scalar(out=var[:], in0=var[:], scalar1=0.0, scalar2=EPS, op0=ALU.max, op1=ALU.add)
         sd = keep.tile(shp, F32, name="sd")
@@ -292,13 +301,13 @@ def tile_modelnew_kernel(
         nc.vector.reciprocal(out=rinv[:], in_=sd[:])
         mg = keep.tile(shp, F32, name="mg")
         nc.vector.tensor_tensor(
-            out=mg[:], in0=mean[:], in1=gsum[:, 0:32].unsqueeze(1).to_broadcast(shp), op=ALU.mult
+            out=mg[:], in0=mean[:], in1=gsum[:, 0:32].unsqueeze(2).to_broadcast(shp), op=ALU.mult
         )
         num = keep.tile(shp, F32, name="num")
         nc.vector.tensor_tensor(out=num[:], in0=s_ps[:, :, :, 1], in1=mg[:], op=ALU.subtract)
         nc.vector.tensor_tensor(out=num[:], in0=num[:], in1=rinv[:], op=ALU.mult)
         tot = keep.tile([P, NJ], F32, name="tot")
-        nc.vector.tensor_reduce(out=tot[:], in_=num[:], axis=AX.X, op=ALU.add)
+        nc.vector.tensor_reduce(out=tot[:], in_=num[:].rearrange("p g j -> p j g"), axis=AX.X, op=ALU.add)
         res = keep.tile([P, NJ], F32, name="res")
         nc.scalar.activation(out=res[:], in_=tot[:], func=ACTF.Relu, bias=gbs[:, 0:1], scale=1.0 / N)
         nc.sync.dma_start(out=out.rearrange("(p j) o -> p (j o)", j=NJ), in_=res[:])

@@ -24,6 +24,8 @@ NPASS = K // 512
 EPS = 1e-5
 NW = 32
 KSPLIT = 3
+LATE = 28
+NL = NG - LATE
 
 FLOPS = 2 * B * K * N
 
@@ -56,8 +58,8 @@ def tile_modelnew_kernel(
 
         x_sb = keep.tile([P, NJ, K], BF16, name="x_sb")
         x_v = x.rearrange("(p j) k -> p j k", j=NJ)
-        for jp in range(NJ // 2):
-            nc.sync.dma_start(out=x_sb[:, 2 * jp : 2 * jp + 2, :], in_=x_v[:, 2 * jp : 2 * jp + 2, :])
+        for j in range(NJ):
+            nc.sync.dma_start(out=x_sb[:, j, :], in_=x_v[:, j, :])
 
         vin = keep.tile([P, P], BF16, name="vin")
         for i, vec in enumerate((bn_weight, bn_bias, gn_weight, gn_bias)):
@@ -65,20 +67,53 @@ def tile_modelnew_kernel(
 
         ws = keep.tile([P, NPASS, N], U8, name="ws", align_bytes=64)
         nc.vector.memset(ws[:].bitcast(I32), 0)
-        for g in range(NPASS):
-            for bq in range(2):
-                for r in range(4):
-                    nc.sync.dma_start(
-                        out=ws[32 * bq + r : P : 64, g, :].bitcast(I32),
-                        in_=weight_scales[g, 4 * bq + r : 16 : 8, :].bitcast(I32),
-                    )
         wq = keep.tile([P, NPASS, 2 * N], U8, name="wq", align_bytes=64)
-        for c in range(4):
+
+        def load_scales(c0, c1):
+            for g in range(NPASS):
+                for bq in range(2):
+                    for r in range(4):
+                        nc.sync.dma_start(
+                            out=ws[32 * bq + r : P : 64, g, c0:c1].bitcast(I32),
+                            in_=weight_scales[g, 4 * bq + r : 16 : 8, c0:c1].bitcast(I32),
+                        )
+
+        def load_words(c0, c1):
             for g in range(NPASS):
                 nc.sync.dma_start(
-                    out=wq[:, g, 2048 * c : 2048 * (c + 1)].bitcast(I32),
-                    in_=weight_words[g, :, 2048 * c : 2048 * (c + 1)].bitcast(I32),
+                    out=wq[:, g, 2 * c0 : 2 * c1].bitcast(I32), in_=weight_words[g, :, 2 * c0 : 2 * c1].bitcast(I32)
                 )
+
+        load_scales(0, 1024)
+        load_words(0, 1024)
+        load_scales(1024, N)
+        load_words(1024, 2048)
+        load_words(2048, 3072)
+        load_words(3072, N)
+
+        x_w = x_sb[:].bitcast(F32)
+        grouped = keep.tile([P, NPASS, 4 * B], BF16, name="grouped", align_bytes=64)
+        grouped_w = grouped[:].bitcast(F32).rearrange("p g (c u) -> p g c u", u=2)
+        xq = keep.tile([P, NPASS, B], U32, name="xq", align_bytes=64)
+        xs = keep.tile([P, NPASS, B], U8, name="xs", align_bytes=64)
+        for j in range(NJ):
+            xt = psy.tile([P, NPASS, 2, P], F32, name="xt", tag="y")
+            for g in range(NPASS):
+                for u in range(2):
+                    nc.tensor.transpose(xt[:, g, u, :], x_w[:, j, 256 * g + u : 256 * (g + 1) : 2], ident[:])
+            dst = grouped_w[:, :, P * j : P * (j + 1), :]
+            src = xt[:].rearrange("p g u c -> p g c u")
+            if j % 2 == 0:
+                nc.vector.tensor_copy(out=dst, in_=src)
+            else:
+                nc.scalar.copy(out=dst, in_=src)
+            if j % 2 == 1:
+                for g in range(NPASS):
+                    nc.vector.quantize_mx(
+                        out=xq[:, g, P * (j - 1) : P * (j + 1)].bitcast(FP8X4),
+                        scales=xs[:, g, P * (j - 1) : P * (j + 1)],
+                        in_=grouped[:, g, 4 * P * (j - 1) : 4 * P * (j + 1)],
+                    )
 
         vT = pst.tile([P, P], BF16, name="vT", tag="gT0")
         nc.tensor.transpose(vT[:], vin[:], ident_bf[:])
@@ -88,11 +123,13 @@ def tile_modelnew_kernel(
         bnb = keep.tile([P, NG], F32, name="bnb")
         nc.vector.tensor_copy(out=bnb[:], in_=vT[:, 32:64])
         rw = keep.tile([P, NG, NW], BF16, name="rw")
-        nc.vector.memset(rw[:], 0.0)
+        nc.gpsimd.memset(rw[:], 0.0)
         nc.vector.memset(rw[:, :, 0], 1.0)
         nc.vector.tensor_copy(out=rw[:, :, 1], in_=vT[:, 64:96])
         rw32 = keep.tile([P, NG, NW], F32, name="rw32")
-        nc.vector.tensor_copy(out=rw32[:], in_=rw[:])
+        nc.gpsimd.memset(rw32[:], 0.0)
+        nc.vector.memset(rw32[:, :, 0], 1.0)
+        nc.vector.tensor_copy(out=rw32[:, :, 1], in_=vT[:, 64:96])
         gwgb = keep.tile([P, 64], BF16, name="gwgb")
         nc.vector.tensor_copy(out=gwgb[:], in_=vT[:, 64:128])
         gsum_ps = pst.tile([P, 64], F32, name="gsum_ps", tag="gT1")
@@ -104,47 +141,16 @@ def tile_modelnew_kernel(
         gbs = keep.tile([P, 1], F32, name="gbs")
         nc.vector.tensor_scalar(out=gbs[:], in0=gbt[:], scalar1=1.0 / N, scalar2=None, op0=ALU.mult)
 
-        x_w = x_sb[:].bitcast(F32)
-        grouped = keep.tile([P, NPASS, 4 * B], BF16, name="grouped", align_bytes=64)
-        grouped_w = grouped[:].bitcast(F32).rearrange("p g (c u) -> p g c u", u=2)
-        xq = keep.tile([P, NPASS, B], U32, name="xq", align_bytes=64)
-        xs = keep.tile([P, NPASS, B], U8, name="xs", align_bytes=64)
-        n_copy = 0
-        for jp in range(NJ // 2):
-            for g in range(NPASS):
-                xt = psy.tile([P, 2, 2, P], F32, name="xt", tag="y")
-                for u in range(2):
-                    for jj in range(2):
-                        nc.tensor.transpose(
-                            xt[:, u, jj, :],
-                            x_w[:, 2 * jp + jj, 256 * g + u : 256 * (g + 1) : 2],
-                            ident[:],
-                        )
-                dst = grouped_w[:, g, 256 * jp : 256 * (jp + 1), :]
-                src = xt[:].rearrange("p u j c -> p (j c) u")
-                if n_copy % 2 == 0:
-                    nc.vector.tensor_copy(out=dst, in_=src)
-                else:
-                    nc.scalar.copy(out=dst, in_=src)
-                n_copy += 1
-            if jp % 2 == 1:
-                hf = jp // 2
-                for g in range(NPASS):
-                    nc.vector.quantize_mx(
-                        out=xq[:, g, 512 * hf : 512 * (hf + 1)].bitcast(FP8X4),
-                        scales=xs[:, g, 512 * hf : 512 * (hf + 1)],
-                        in_=grouped[:, g, 2048 * hf : 2048 * (hf + 1)],
-                    )
-
-        s_ps = pss.tile([P, NG, NJ, 2], F32, name="s_ps")
-        s_flat = s_ps[:].rearrange("p g j c -> p (g j c)")
-        s2 = keep.tile([P, NG, 4], F32, name="s2")
-        st2 = keep.tile([P, NG, 4, 6], F32, name="st2")
+        s_ps = pss.tile([P, 512], F32, name="s_ps")
+        s2 = keep.tile([P, LATE, 4], F32, name="s2")
+        st2 = keep.tile([P, LATE, 4, 6], F32, name="st2")
+        st2l = keep.tile([P, NL, NJ, 6], F32, name="st2l")
         ys = {}
         coef = {}
         acts = {}
         stats = {}
         gts = {}
+        late = {}
 
         def stage_mx(G):
             y = []
@@ -203,11 +209,15 @@ def tile_modelnew_kernel(
             acts[G] = g32
 
         def stage_hi(G):
+            if G >= LATE:
+                return
             hi = work.tile([P, P * KSPLIT], BF16, name="hi")
             nc.vector.tensor_copy(out=hi[:], in_=acts[G][:, 0 : P * KSPLIT])
             coef[G] = hi
 
         def stage_lo(G):
+            if G >= LATE:
+                return
             hi = coef[G]
             lo = work.tile([P, P * KSPLIT], BF16, name="lo")
             nc.vector.tensor_tensor(out=lo[:], in0=acts[G][:, 0 : P * KSPLIT], in1=hi[:], op=ALU.subtract)
@@ -225,29 +235,111 @@ def tile_modelnew_kernel(
             gts[G] = tiles
 
         def stage_square_act(G):
+            if G >= LATE:
+                return
             gT = gts[G][0]
             for q in range(4):
                 junk = small.tile([P, P], BF16, name="junk")
                 nc.scalar.activation(out=junk[:], in_=gT[:, q, :], func=ACTF.Square, accum_out=s2[:, G, q : q + 1])
 
         def stage_square_dve(G):
+            if G >= LATE:
+                for j in range(NJ):
+                    nc.vector.bn_stats(out=st2l[:, G - LATE, j, :], in_=gts[G][j // 4][:, j % 4, :])
+                return
             gT = gts[G][1]
             for q in range(4):
                 nc.vector.bn_stats(out=st2[:, G, q, :], in_=gT[:, q, :])
 
         def stage_sums(G):
             g32 = acts[G]
-            hi, lo = coef[G]
+            if G == LATE:
+                late[0] = psy.tile([P, 512], F32, name="s_late", tag="y")
             for j in range(NJ):
                 cols = slice(P * j, P * (j + 1))
-                first = 2 * (NJ * G + j)
-                width = min(NW, 512 - first)
-                dst = s_flat[:, first : first + width]
-                if j < KSPLIT:
-                    nc.tensor.matmul(dst, lhsT=hi[:, cols], rhs=rw[:, G, 0:width], start=True, stop=False)
-                    nc.tensor.matmul(dst, lhsT=lo[:, cols], rhs=rw[:, G, 0:width], start=False, stop=True)
+                if G < LATE:
+                    first = 2 * (NJ * G + j)
+                    dst = s_ps[:, first : first + NW]
                 else:
-                    nc.tensor.matmul(dst, lhsT=g32[:, cols], rhs=rw32[:, G, 0:width], start=True, stop=True)
+                    first = 2 * (NJ * (G - LATE) + j)
+                    dst = late[0][:, first : first + NW]
+                if G < LATE and j < KSPLIT:
+                    hi, lo = coef[G]
+                    nc.tensor.matmul(dst, lhsT=hi[:, cols], rhs=rw[:, G, :], start=True, stop=False)
+                    nc.tensor.matmul(dst, lhsT=lo[:, cols], rhs=rw[:, G, :], start=False, stop=True)
+                else:
+                    nc.tensor.matmul(dst, lhsT=g32[:, cols], rhs=rw32[:, G, :], start=True, stop=True)
+
+        con = keep.tile([P, NJ, NL + 1], F32, name="con")
+        fin = {}
+
+        def finish_numerator(key, sums, g0, n_g):
+            shp = [P, n_g, NJ]
+            sv = sums[:, 0 : 2 * NJ * n_g].rearrange("p (g j c) -> p g j c", j=NJ, c=2)
+            mean = keep.tile(shp, F32, name="mean" + key)
+            nc.vector.tensor_scalar(out=mean[:], in0=sv[:, :, :, 0], scalar1=1.0 / P, scalar2=None, op0=ALU.mult)
+            mg = keep.tile(shp, F32, name="mg" + key)
+            nc.vector.tensor_tensor(
+                out=mg[:], in0=mean[:], in1=gsum[:, g0 : g0 + n_g].unsqueeze(2).to_broadcast(shp), op=ALU.mult
+            )
+            num = keep.tile(shp, F32, name="num" + key)
+            nc.vector.tensor_tensor(out=num[:], in0=sv[:, :, :, 1], in1=mg[:], op=ALU.subtract)
+            fin["mean" + key] = mean
+            fin["num" + key] = num
+
+        def variance_from_stats(key, st, dst, shp):
+            dd = keep.tile(shp, F32, name="dd" + key)
+            nc.vector.tensor_tensor(out=dd[:], in0=st[:, :, :, 1], in1=st[:, :, :, 4], op=ALU.subtract)
+            m2 = keep.tile(shp, F32, name="m2" + key)
+            nc.vector.tensor_tensor(out=m2[:], in0=st[:, :, :, 2], in1=st[:, :, :, 5], op=ALU.add)
+            dq = keep.tile(shp, F32, name="dq" + key)
+            nc.vector.scalar_tensor_tensor(out=dq[:], in0=dd[:], scalar=0.25, in1=dd[:], op0=ALU.mult, op1=ALU.mult)
+            nc.vector.tensor_scalar(out=m2[:], in0=m2[:], scalar1=1.0 / P, scalar2=EPS, op0=ALU.mult, op1=ALU.add)
+            nc.vector.tensor_tensor(out=dst, in0=m2[:], in1=dq[:], op=ALU.add)
+
+        def finish_early_a():
+            finish_numerator("e", s_ps, 0, LATE)
+            var = keep.tile([P, LATE, NJ], F32, name="var_e")
+            variance_from_stats("e", st2, var[:, :, 4:8], [P, LATE, 4])
+            mean = fin["meane"]
+            msq = keep.tile([P, LATE, 4], F32, name="msq")
+            nc.vector.tensor_tensor(out=msq[:], in0=mean[:, :, 0:4], in1=mean[:, :, 0:4], op=ALU.mult)
+            nc.vector.scalar_tensor_tensor(
+                out=var[:, :, 0:4], in0=s2[:], scalar=1.0 / P, in1=msq[:], op0=ALU.mult, op1=ALU.subtract
+            )
+            nc.vector.tensor_scalar(
+                out=var[:, :, 0:4], in0=var[:, :, 0:4], scalar1=0.0, scalar2=EPS, op0=ALU.max, op1=ALU.add
+            )
+            fin["vare"] = var
+
+        def finish_sqrt(key, shp):
+            sd = keep.tile(shp, F32, name="sd" + key)
+            nc.scalar.activation(out=sd[:], in_=fin["var" + key][:], func=ACTF.Sqrt)
+            fin["sd" + key] = sd
+
+        def finish_early_b():
+            rinv = keep.tile([P, LATE, NJ], F32, name="rinv_e")
+            nc.vector.reciprocal(out=rinv[:], in_=fin["sde"][:])
+            num = fin["nume"]
+            nc.vector.tensor_tensor(out=num[:], in0=num[:], in1=rinv[:], op=ALU.mult)
+            nc.vector.tensor_reduce(out=con[:, :, NL], in_=num[:].rearrange("p g j -> p j g"), axis=AX.X, op=ALU.add)
+
+        def finish_late_a():
+            var = keep.tile([P, NL, NJ], F32, name="var_l")
+            variance_from_stats("l", st2l, var[:], [P, NL, NJ])
+            fin["varl"] = var
+
+        def finish_late_b():
+            rinv = keep.tile([P, NL, NJ], F32, name="rinv_l")
+            nc.vector.reciprocal(out=rinv[:], in_=fin["sdl"][:])
+            nc.vector.tensor_tensor(
+                out=con[:, :, 0:NL].rearrange("p j g -> p g j"), in0=fin["numl"][:], in1=rinv[:], op=ALU.mult
+            )
+            tot = keep.tile([P, NJ], F32, name="tot")
+            nc.vector.tensor_reduce(out=tot[:], in_=con[:], axis=AX.X, op=ALU.add)
+            res = keep.tile([P, NJ], F32, name="res")
+            nc.scalar.activation(out=res[:], in_=tot[:], func=ACTF.Relu, bias=gbs[:, 0:1], scale=1.0 / N)
+            nc.sync.dma_start(out=out.rearrange("(p j) o -> p (j o)", j=NJ), in_=res[:])
 
         def live(G):
             return 0 <= G < NG
@@ -257,6 +349,10 @@ def tile_modelnew_kernel(
                 if live(T - 3):
                     stage_square_dve(T - 3)
                     stage_square_act(T - 3)
+                if T == NG:
+                    finish_early_a()
+                if T == NG + 1:
+                    finish_early_b()
                 if live(T):
                     stage_mx(T)
                     stage_stats(T)
@@ -270,44 +366,13 @@ def tile_modelnew_kernel(
                     stage_eps(T)
                 if live(T - 1):
                     stage_gelu(T - 1)
+                if T == NG:
+                    finish_sqrt("e", [P, LATE, NJ])
                 if live(T - 2):
                     stage_transpose(T - 2)
                 if live(T - 3):
                     stage_sums(T - 3)
-
-        shp = [P, NG, NJ]
-        half = [P, NG, 4]
-        mean = keep.tile(shp, F32, name="mean")
-        nc.vector.tensor_scalar(out=mean[:], in0=s_ps[:, :, :, 0], scalar1=1.0 / P, scalar2=None, op0=ALU.mult)
-        var = keep.tile(shp, F32, name="var")
-        dd = keep.tile(half, F32, name="dd")
-        nc.vector.tensor_tensor(out=dd[:], in0=st2[:, :, :, 1], in1=st2[:, :, :, 4], op=ALU.subtract)
-        dq = keep.tile(half, F32, name="dq")
-        nc.vector.scalar_tensor_tensor(out=dq[:], in0=dd[:], scalar=0.25, in1=dd[:], op0=ALU.mult, op1=ALU.mult)
-        m2 = keep.tile(half, F32, name="m2")
-        nc.vector.tensor_tensor(out=m2[:], in0=st2[:, :, :, 2], in1=st2[:, :, :, 5], op=ALU.add)
-        nc.vector.scalar_tensor_tensor(
-            out=var[:, :, 4:8], in0=m2[:], scalar=1.0 / P, in1=dq[:], op0=ALU.mult, op1=ALU.add
-        )
-        msq = keep.tile(half, F32, name="msq")
-        nc.vector.tensor_tensor(out=msq[:], in0=mean[:, :, 0:4], in1=mean[:, :, 0:4], op=ALU.mult)
-        nc.vector.scalar_tensor_tensor(
-            out=var[:, :, 0:4], in0=s2[:], scalar=1.0 / P, in1=msq[:], op0=ALU.mult, op1=ALU.subtract
-        )
-        nc.vector.tensor_scalar(out=var[:], in0=var[:], scalar1=0.0, scalar2=EPS, op0=ALU.max, op1=ALU.add)
-        sd = keep.tile(shp, F32, name="sd")
-        nc.scalar.activation(out=sd[:], in_=var[:], func=ACTF.Sqrt)
-        rinv = keep.tile(shp, F32, name="rinv")
-        nc.vector.reciprocal(out=rinv[:], in_=sd[:])
-        mg = keep.tile(shp, F32, name="mg")
-        nc.vector.tensor_tensor(
-            out=mg[:], in0=mean[:], in1=gsum[:, 0:32].unsqueeze(2).to_broadcast(shp), op=ALU.mult
-        )
-        num = keep.tile(shp, F32, name="num")
-        nc.vector.tensor_tensor(out=num[:], in0=s_ps[:, :, :, 1], in1=mg[:], op=ALU.subtract)
-        nc.vector.tensor_tensor(out=num[:], in0=num[:], in1=rinv[:], op=ALU.mult)
-        tot = keep.tile([P, NJ], F32, name="tot")
-        nc.vector.tensor_reduce(out=tot[:], in_=num[:].rearrange("p g j -> p j g"), axis=AX.X, op=ALU.add)
-        res = keep.tile([P, NJ], F32, name="res")
-        nc.scalar.activation(out=res[:], in_=tot[:], func=ACTF.Relu, bias=gbs[:, 0:1], scale=1.0 / N)
-        nc.sync.dma_start(out=out.rearrange("(p j) o -> p (j o)", j=NJ), in_=res[:])
+            finish_late_a()
+            finish_sqrt("l", [P, NL, NJ])
+            finish_numerator("l", late[0], LATE, NL)
+            finish_late_b()

@@ -23,7 +23,8 @@ NJ = B // P
 NPASS = K // 512
 EPS = 1e-5
 NW = 32
-KSPLIT = 3
+KD = 3
+KA = 4
 LATE = 28
 NL = NG - LATE
 
@@ -37,7 +38,7 @@ def tile_modelnew_kernel(
     assert num_groups == NG
     with ExitStack() as ctx:
         keep = ctx.enter_context(tc.tile_pool(name="keep", bufs=1))
-        work = ctx.enter_context(tc.tile_pool(name="work", bufs=5))
+        work = ctx.enter_context(tc.tile_pool(name="work", bufs=6))
         small = ctx.enter_context(tc.tile_pool(name="small", bufs=6))
         psy = ctx.enter_context(tc.psum_pool(name="psy", bufs=5))
         pst = ctx.enter_context(tc.psum_pool(name="pst", bufs=1))
@@ -151,6 +152,7 @@ def tile_modelnew_kernel(
         stats = {}
         gts = {}
         late = {}
+        parts = {}
 
         def stage_mx(G):
             y = []
@@ -209,19 +211,29 @@ def tile_modelnew_kernel(
             acts[G] = g32
 
         def stage_hi(G):
-            if G >= LATE:
-                return
-            hi = work.tile([P, P * KSPLIT], BF16, name="hi")
-            nc.vector.tensor_copy(out=hi[:], in_=acts[G][:, 0 : P * KSPLIT])
+            hi = work.tile([P, P * KD], BF16, name="hi")
+            nc.vector.tensor_copy(out=hi[:], in_=acts[G][:, 0 : P * KD])
             coef[G] = hi
 
         def stage_lo(G):
-            if G >= LATE:
-                return
             hi = coef[G]
-            lo = work.tile([P, P * KSPLIT], BF16, name="lo")
-            nc.vector.tensor_tensor(out=lo[:], in0=acts[G][:, 0 : P * KSPLIT], in1=hi[:], op=ALU.subtract)
+            lo = work.tile([P, P * KD], BF16, name="lo")
+            nc.vector.tensor_tensor(out=lo[:], in0=acts[G][:, 0 : P * KD], in1=hi[:], op=ALU.subtract)
             coef[G] = (hi, lo)
+
+        def stage_hi_act(G):
+            hia = work.tile([P, P * KA], BF16, name="hia")
+            nc.scalar.copy(out=hia[:], in_=acts[G][:, P * KD : P * (KD + KA)])
+            loa = work.tile([P, P * KA], BF16, name="loa")
+            parts[G] = (hia, loa)
+
+        def stage_lo_pool(G):
+            hia, loa = parts[G]
+            half = P * KA // 2
+            for i in range(2):
+                cols = slice(half * i, half * (i + 1))
+                src = slice(P * KD + half * i, P * KD + half * (i + 1))
+                nc.gpsimd.tensor_tensor(out=loa[:, cols], in0=acts[G][:, src], in1=hia[:, cols], op=ALU.subtract)
 
         def stage_transpose(G):
             g32 = acts[G]
@@ -263,8 +275,11 @@ def tile_modelnew_kernel(
                 else:
                     first = 2 * (NJ * (G - LATE) + j)
                     dst = late[0][:, first : first + NW]
-                if G < LATE and j < KSPLIT:
+                if j < KD + KA:
                     hi, lo = coef[G]
+                    if j >= KD:
+                        hi, lo = parts[G]
+                        cols = slice(P * (j - KD), P * (j - KD + 1))
                     nc.tensor.matmul(dst, lhsT=hi[:, cols], rhs=rw[:, G, :], start=True, stop=False)
                     nc.tensor.matmul(dst, lhsT=lo[:, cols], rhs=rw[:, G, :], start=False, stop=True)
                 else:
@@ -345,10 +360,14 @@ def tile_modelnew_kernel(
             return 0 <= G < NG
 
         with tc.manual_schedule():
-            for T in range(NG + 3):
+            for T in range(NG + 4):
                 if live(T - 3):
                     stage_square_dve(T - 3)
                     stage_square_act(T - 3)
+                if live(T - 2):
+                    stage_hi_act(T - 2)
+                if live(T - 3):
+                    stage_lo_pool(T - 3)
                 if T == NG:
                     finish_early_a()
                 if T == NG + 1:
@@ -370,8 +389,8 @@ def tile_modelnew_kernel(
                     finish_sqrt("e", [P, LATE, NJ])
                 if live(T - 2):
                     stage_transpose(T - 2)
-                if live(T - 3):
-                    stage_sums(T - 3)
+                if live(T - 4):
+                    stage_sums(T - 4)
             finish_late_a()
             finish_sqrt("l", [P, NL, NJ])
             finish_numerator("l", late[0], LATE, NL)

@@ -38,7 +38,7 @@ def tile_modelnew_kernel(
     assert num_groups == NG
     with ExitStack() as ctx:
         keep = ctx.enter_context(tc.tile_pool(name="keep", bufs=1))
-        work = ctx.enter_context(tc.tile_pool(name="work", bufs=6))
+        work = ctx.enter_context(tc.tile_pool(name="work", bufs=7))
         small = ctx.enter_context(tc.tile_pool(name="small", bufs=6))
         psy = ctx.enter_context(tc.psum_pool(name="psy", bufs=5))
         pst = ctx.enter_context(tc.psum_pool(name="pst", bufs=1))
@@ -189,6 +189,10 @@ def tile_modelnew_kernel(
             nc.vector.tensor_scalar(out=ve[:], in0=mv[:, 1:2], scalar1=EPS, scalar2=None, op0=ALU.add)
             mb = small.tile([P, 1], F32, name="mb")
             nc.vector.tensor_tensor(out=mb[:], in0=mv[:, 0:1], in1=bw2[:, G, 1:2], op=ALU.mult)
+            stats[G] = (ve, mb)
+
+        def stage_pow(G):
+            ve, mb = stats[G]
             rstd = small.tile([P, 1], F32, name="rstd")
             nc.gpsimd.tensor_tensor(out=rstd[:], in0=ve[:], in1=mhalf[:], op=ALU.pow)
             stats[G] = (rstd, mb)
@@ -227,41 +231,33 @@ def tile_modelnew_kernel(
             loa = work.tile([P, P * KA], BF16, name="loa")
             parts[G] = (hia, loa)
 
-        def stage_lo_pool(G):
+        def stage_lo_pool(G, i):
             hia, loa = parts[G]
             half = P * KA // 2
-            for i in range(2):
-                cols = slice(half * i, half * (i + 1))
-                src = slice(P * KD + half * i, P * KD + half * (i + 1))
-                nc.gpsimd.tensor_tensor(out=loa[:, cols], in0=acts[G][:, src], in1=hia[:, cols], op=ALU.subtract)
+            cols = slice(half * i, half * (i + 1))
+            src = slice(P * KD + half * i, P * KD + half * (i + 1))
+            nc.gpsimd.tensor_tensor(out=loa[:, cols], in0=acts[G][:, src], in1=hia[:, cols], op=ALU.subtract)
 
-        def stage_transpose(G):
+        def stage_transpose(G, hf):
             g32 = acts[G]
-            tiles = []
-            for hf in range(2):
-                gT = pst.tile([P, 4, P], F32, name="gT%d" % hf)
-                for q in range(4):
-                    j = 4 * hf + q
-                    nc.tensor.transpose(gT[:, q, :], g32[:, P * j : P * (j + 1)], ident[:])
-                tiles.append(gT)
-            gts[G] = tiles
-
-        def stage_square_act(G):
-            if G >= LATE:
-                return
-            gT = gts[G][0]
+            gT = pst.tile([P, 4, P], F32, name="gT%d" % hf)
             for q in range(4):
-                junk = small.tile([P, P], BF16, name="junk")
-                nc.scalar.activation(out=junk[:], in_=gT[:, q, :], func=ACTF.Square, accum_out=s2[:, G, q : q + 1])
+                j = 4 * hf + q
+                nc.tensor.transpose(gT[:, q, :], g32[:, P * j : P * (j + 1)], ident[:])
+            gts[(G, hf)] = gT
 
-        def stage_square_dve(G):
-            if G >= LATE:
-                for j in range(NJ):
-                    nc.vector.bn_stats(out=st2l[:, G - LATE, j, :], in_=gts[G][j // 4][:, j % 4, :])
-                return
-            gT = gts[G][1]
+        def stage_square(G, hf):
+            gT = gts[(G, hf)]
             for q in range(4):
-                nc.vector.bn_stats(out=st2[:, G, q, :], in_=gT[:, q, :])
+                if G >= LATE:
+                    nc.vector.bn_stats(out=st2l[:, G - LATE, 4 * hf + q, :], in_=gT[:, q, :])
+                elif hf == 1:
+                    nc.vector.bn_stats(out=st2[:, G, q, :], in_=gT[:, q, :])
+                else:
+                    junk = small.tile([P, P], BF16, name="junk")
+                    nc.scalar.activation(
+                        out=junk[:], in_=gT[:, q, :], func=ACTF.Square, accum_out=s2[:, G, q : q + 1]
+                    )
 
         def stage_sums(G):
             g32 = acts[G]
@@ -360,37 +356,41 @@ def tile_modelnew_kernel(
             return 0 <= G < NG
 
         with tc.manual_schedule():
-            for T in range(NG + 4):
+            for T in range(NG + 6):
+                if live(T - 5):
+                    stage_sums(T - 5)
                 if live(T - 3):
-                    stage_square_dve(T - 3)
-                    stage_square_act(T - 3)
+                    stage_transpose(T - 3, 0)
                 if live(T - 2):
                     stage_hi_act(T - 2)
                 if live(T - 3):
-                    stage_lo_pool(T - 3)
+                    stage_square(T - 3, 0)
+                if live(T - 2):
+                    stage_lo_pool(T - 2, 0)
+                if live(T - 4):
+                    stage_square(T - 4, 1)
+                    stage_lo(T - 4)
+                if live(T):
+                    stage_mx(T)
+                if live(T - 3):
+                    stage_transpose(T - 3, 1)
+                if live(T):
+                    stage_stats(T)
+                    stage_aggr(T)
+                    stage_eps(T)
+                    stage_pow(T)
                 if T == NG:
                     finish_early_a()
                 if T == NG + 1:
                     finish_early_b()
-                if live(T):
-                    stage_mx(T)
-                    stage_stats(T)
                 if live(T - 2):
-                    stage_hi(T - 2)
-                if live(T):
-                    stage_aggr(T)
-                if live(T - 2):
-                    stage_lo(T - 2)
-                if live(T):
-                    stage_eps(T)
+                    stage_lo_pool(T - 2, 1)
                 if live(T - 1):
                     stage_gelu(T - 1)
                 if T == NG:
                     finish_sqrt("e", [P, LATE, NJ])
-                if live(T - 2):
-                    stage_transpose(T - 2)
-                if live(T - 4):
-                    stage_sums(T - 4)
+                if live(T - 3):
+                    stage_hi(T - 3)
             finish_late_a()
             finish_sqrt("l", [P, NL, NJ])
             finish_numerator("l", late[0], LATE, NL)

@@ -23,8 +23,7 @@ NJ = B // P
 NPASS = K // 512
 EPS = 1e-5
 NW = 32
-KD = 3
-KA = 4
+KA = 6
 LATE = 28
 NL = NG - LATE
 
@@ -143,11 +142,8 @@ def tile_modelnew_kernel(
         nc.vector.tensor_scalar(out=gbs[:], in0=gbt[:], scalar1=1.0 / N, scalar2=None, op0=ALU.mult)
 
         s_ps = pss.tile([P, 512], F32, name="s_ps")
-        s2 = keep.tile([P, LATE, 4], F32, name="s2")
-        st2 = keep.tile([P, LATE, 4, 6], F32, name="st2")
-        st2l = keep.tile([P, NL, NJ, 6], F32, name="st2l")
+        st2 = keep.tile([P, NG, NJ, 6], F32, name="st2")
         ys = {}
-        coef = {}
         acts = {}
         stats = {}
         gts = {}
@@ -214,20 +210,9 @@ def tile_modelnew_kernel(
                 )
             acts[G] = g32
 
-        def stage_hi(G):
-            hi = work.tile([P, P * KD], BF16, name="hi")
-            nc.vector.tensor_copy(out=hi[:], in_=acts[G][:, 0 : P * KD])
-            coef[G] = hi
-
-        def stage_lo(G):
-            hi = coef[G]
-            lo = work.tile([P, P * KD], BF16, name="lo")
-            nc.vector.tensor_tensor(out=lo[:], in0=acts[G][:, 0 : P * KD], in1=hi[:], op=ALU.subtract)
-            coef[G] = (hi, lo)
-
         def stage_hi_act(G):
             hia = work.tile([P, P * KA], BF16, name="hia")
-            nc.scalar.copy(out=hia[:], in_=acts[G][:, P * KD : P * (KD + KA)])
+            nc.scalar.copy(out=hia[:], in_=acts[G][:, 0 : P * KA])
             loa = work.tile([P, P * KA], BF16, name="loa")
             parts[G] = (hia, loa)
 
@@ -235,8 +220,7 @@ def tile_modelnew_kernel(
             hia, loa = parts[G]
             half = P * KA // 2
             cols = slice(half * i, half * (i + 1))
-            src = slice(P * KD + half * i, P * KD + half * (i + 1))
-            nc.gpsimd.tensor_tensor(out=loa[:, cols], in0=acts[G][:, src], in1=hia[:, cols], op=ALU.subtract)
+            nc.gpsimd.tensor_tensor(out=loa[:, cols], in0=acts[G][:, cols], in1=hia[:, cols], op=ALU.subtract)
 
         def stage_transpose(G, hf):
             g32 = acts[G]
@@ -246,18 +230,10 @@ def tile_modelnew_kernel(
                 nc.tensor.transpose(gT[:, q, :], g32[:, P * j : P * (j + 1)], ident[:])
             gts[(G, hf)] = gT
 
-        def stage_square(G, hf):
+        def stage_square(G, hf, q0, q1):
             gT = gts[(G, hf)]
-            for q in range(4):
-                if G >= LATE:
-                    nc.vector.bn_stats(out=st2l[:, G - LATE, 4 * hf + q, :], in_=gT[:, q, :])
-                elif hf == 1:
-                    nc.vector.bn_stats(out=st2[:, G, q, :], in_=gT[:, q, :])
-                else:
-                    junk = small.tile([P, P], BF16, name="junk")
-                    nc.scalar.activation(
-                        out=junk[:], in_=gT[:, q, :], func=ACTF.Square, accum_out=s2[:, G, q : q + 1]
-                    )
+            for q in range(q0, q1):
+                nc.vector.bn_stats(out=st2[:, G, 4 * hf + q, :], in_=gT[:, q, :])
 
         def stage_sums(G):
             g32 = acts[G]
@@ -271,11 +247,8 @@ def tile_modelnew_kernel(
                 else:
                     first = 2 * (NJ * (G - LATE) + j)
                     dst = late[0][:, first : first + NW]
-                if j < KD + KA:
-                    hi, lo = coef[G]
-                    if j >= KD:
-                        hi, lo = parts[G]
-                        cols = slice(P * (j - KD), P * (j - KD + 1))
+                if j < KA:
+                    hi, lo = parts[G]
                     nc.tensor.matmul(dst, lhsT=hi[:, cols], rhs=rw[:, G, :], start=True, stop=False)
                     nc.tensor.matmul(dst, lhsT=lo[:, cols], rhs=rw[:, G, :], start=False, stop=True)
                 else:
@@ -311,16 +284,7 @@ def tile_modelnew_kernel(
         def finish_early_a():
             finish_numerator("e", s_ps, 0, LATE)
             var = keep.tile([P, LATE, NJ], F32, name="var_e")
-            variance_from_stats("e", st2, var[:, :, 4:8], [P, LATE, 4])
-            mean = fin["meane"]
-            msq = keep.tile([P, LATE, 4], F32, name="msq")
-            nc.vector.tensor_tensor(out=msq[:], in0=mean[:, :, 0:4], in1=mean[:, :, 0:4], op=ALU.mult)
-            nc.vector.scalar_tensor_tensor(
-                out=var[:, :, 0:4], in0=s2[:], scalar=1.0 / P, in1=msq[:], op0=ALU.mult, op1=ALU.subtract
-            )
-            nc.vector.tensor_scalar(
-                out=var[:, :, 0:4], in0=var[:, :, 0:4], scalar1=0.0, scalar2=EPS, op0=ALU.max, op1=ALU.add
-            )
+            variance_from_stats("e", st2[:, 0:LATE, :, :], var[:], [P, LATE, NJ])
             fin["vare"] = var
 
         def finish_sqrt(key, shp):
@@ -337,7 +301,7 @@ def tile_modelnew_kernel(
 
         def finish_late_a():
             var = keep.tile([P, NL, NJ], F32, name="var_l")
-            variance_from_stats("l", st2l, var[:], [P, NL, NJ])
+            variance_from_stats("l", st2[:, LATE:NG, :, :], var[:], [P, NL, NJ])
             fin["varl"] = var
 
         def finish_late_b():
@@ -356,42 +320,39 @@ def tile_modelnew_kernel(
             return 0 <= G < NG
 
         with tc.manual_schedule():
-            for T in range(NG + 6):
-                if live(T - 5):
-                    stage_sums(T - 5)
-                if live(T - 3):
-                    stage_transpose(T - 3, 0)
+            for T in range(NG + 5):
+                if live(T - 4):
+                    stage_square(T - 4, 1, 0, 4)
                 if live(T - 2):
                     stage_hi_act(T - 2)
                 if live(T - 3):
-                    stage_square(T - 3, 0)
-                if live(T - 2):
-                    stage_lo_pool(T - 2, 0)
-                if live(T - 4):
-                    stage_square(T - 4, 1)
-                    stage_lo(T - 4)
+                    stage_lo_pool(T - 3, 0)
+                    stage_lo_pool(T - 3, 1)
                 if live(T):
                     stage_mx(T)
                 if live(T - 3):
+                    stage_transpose(T - 3, 0)
                     stage_transpose(T - 3, 1)
+                if live(T - 4):
+                    stage_sums(T - 4)
                 if live(T):
                     stage_stats(T)
                     stage_aggr(T)
+                if live(T - 3):
+                    stage_square(T - 3, 0, 0, 2)
+                if live(T):
                     stage_eps(T)
                     stage_pow(T)
+                if live(T - 3):
+                    stage_square(T - 3, 0, 2, 4)
                 if T == NG:
                     finish_early_a()
-                if T == NG + 1:
-                    finish_early_b()
-                if live(T - 2):
-                    stage_lo_pool(T - 2, 1)
                 if live(T - 1):
                     stage_gelu(T - 1)
                 if T == NG:
                     finish_sqrt("e", [P, LATE, NJ])
-                if live(T - 3):
-                    stage_hi(T - 3)
             finish_late_a()
             finish_sqrt("l", [P, NL, NJ])
+            finish_early_b()
             finish_numerator("l", late[0], LATE, NL)
             finish_late_b()

@@ -103,7 +103,7 @@ def tile_modelnew_kernel(
                     nc.tensor.transpose(xt[:, g, u, :], x_w[:, j, 256 * g + u : 256 * (g + 1) : 2], ident[:])
             dst = grouped_w[:, :, P * j : P * (j + 1), :]
             src = xt[:].rearrange("p g u c -> p g c u")
-            if j % 2 == 0:
+            if j % 2 == 1:
                 nc.vector.tensor_copy(out=dst, in_=src)
             else:
                 nc.scalar.copy(out=dst, in_=src)
@@ -211,12 +211,16 @@ def tile_modelnew_kernel(
             acts[G] = g32
 
         def stage_hi_act(G):
+            if G == NG - 1:
+                return
             hia = work.tile([P, P * KA], BF16, name="hia")
             nc.scalar.copy(out=hia[:], in_=acts[G][:, 0 : P * KA])
             loa = work.tile([P, P * KA], BF16, name="loa")
             parts[G] = (hia, loa)
 
         def stage_lo_pool(G, i):
+            if G == NG - 1:
+                return
             hia, loa = parts[G]
             half = P * KA // 2
             cols = slice(half * i, half * (i + 1))
@@ -247,7 +251,7 @@ def tile_modelnew_kernel(
                 else:
                     first = 2 * (NJ * (G - LATE) + j)
                     dst = late[0][:, first : first + NW]
-                if j < KA:
+                if j < KA and G < NG - 1:
                     hi, lo = parts[G]
                     nc.tensor.matmul(dst, lhsT=hi[:, cols], rhs=rw[:, G, :], start=True, stop=False)
                     nc.tensor.matmul(dst, lhsT=lo[:, cols], rhs=rw[:, G, :], start=False, stop=True)

from contextlib import ExitStack

import concourse.mybir as mybir
from concourse.masks import make_identity

F32 = mybir.dt.float32
BF16 = mybir.dt.bfloat16
U8 = mybir.dt.uint8
U32 = mybir.dt.uint32
I32 = mybir.dt.int32
FP8X4 = mybir.dt.float8_e4m3fn_x4
FP4X4 = mybir.dt.float4_e2m1fn_x4
ACTF = mybir.ActivationFunctionType
ALU = mybir.AluOpType
AX = mybir.AxisListType

P = 128
B = 1024
K = 1024
N = 4096
NG = 32
NJ = B // P
NPASS = K // 512
EPS = 1e-5
NW = 32
KA = 6
LATE = 28
NL = NG - LATE

FLOPS = 2 * B * K * N


def tile_modelnew_kernel(
    tc, x, weight_words, weight_scales, bias, bn_weight, bn_bias, gn_weight, gn_bias, num_groups, out
):
    nc = tc.nc
    assert num_groups == NG
    with ExitStack() as ctx:
        keep = ctx.enter_context(tc.tile_pool(name="keep", bufs=1))
        work = ctx.enter_context(tc.tile_pool(name="work", bufs=7))
        small = ctx.enter_context(tc.tile_pool(name="small", bufs=6))
        psy = ctx.enter_context(tc.psum_pool(name="psy", bufs=5))
        pst = ctx.enter_context(tc.psum_pool(name="pst", bufs=1))
        pss = ctx.enter_context(tc.psum_pool(name="pss", bufs=1))

        ident = keep.tile([P, P], F32, name="ident")
        make_identity(nc, ident[:])
        ident_bf = keep.tile([P, P], BF16, name="ident_bf")
        nc.vector.tensor_copy(out=ident_bf[:], in_=ident[:])
        ones_bf = keep.tile([P, P], BF16, name="ones_bf")
        nc.vector.memset(ones_bf[:], 1.0)
        mhalf = keep.tile([P, 1], F32, name="mhalf")
        nc.vector.memset(mhalf[:], -0.5)
        zero1 = keep.tile([P, 1], F32, name="zero1")
        nc.vector.memset(zero1[:], 0.0)
        warm = keep.tile([P, 1], F32, name="warm")
        nc.scalar.activation(out=warm[:], in_=zero1[:], func=ACTF.Gelu)

        x_sb = keep.tile([P, NJ, K], BF16, name="x_sb")
        x_v = x.rearrange("(p j) k -> p j k", j=NJ)
        for j in range(NJ):
            nc.sync.dma_start(out=x_sb[:, j, :], in_=x_v[:, j, :])

        vin = keep.tile([P, P], BF16, name="vin")
        for i, vec in enumerate((bn_weight, bn_bias, gn_weight, gn_bias)):
            nc.scalar.dma_start(out=vin[32 * i : 32 * i + 32, :], in_=vec.rearrange("(g c) -> g c", c=P))

        ws = keep.tile([P, NPASS, N], U8, name="ws", align_bytes=64)
        nc.vector.memset(ws[:].bitcast(I32), 0)
        wq = keep.tile([P, NPASS, 2 * N], U8, name="wq", align_bytes=64)

        def load_scales(c0, c1):
            for g in range(NPASS):
                for bq in range(2):
                    for r in range(4):
                        nc.sync.dma_start(
                            out=ws[32 * bq + r : P : 64, g, c0:c1].bitcast(I32),
                            in_=weight_scales[g, 4 * bq + r : 16 : 8, c0:c1].bitcast(I32),
                        )

        def load_words(c0, c1):
            for g in range(NPASS):
                nc.sync.dma_start(
                    out=wq[:, g, 2 * c0 : 2 * c1].bitcast(I32), in_=weight_words[g, :, 2 * c0 : 2 * c1].bitcast(I32)
                )

        load_scales(0, 1024)
        load_words(0, 1024)
        load_scales(1024, N)
        load_words(1024, 2048)
        load_words(2048, 3072)
        load_words(3072, N)

        x_w = x_sb[:].bitcast(F32)
        grouped = keep.tile([P, NPASS, 4 * B], BF16, name="grouped", align_bytes=64)
        grouped_w = grouped[:].bitcast(F32).rearrange("p g (c u) -> p g c u", u=2)
        xq = keep.tile([P, NPASS, B], U32, name="xq", align_bytes=64)
        xs = keep.tile([P, NPASS, B], U8, name="xs", align_bytes=64)
        for j in range(NJ):
            xt = psy.tile([P, NPASS, 2, P], F32, name="xt", tag="y")
            for g in range(NPASS):
                for u in range(2):
                    nc.tensor.transpose(xt[:, g, u, :], x_w[:, j, 256 * g + u : 256 * (g + 1) : 2], ident[:])
            dst = grouped_w[:, :, P * j : P * (j + 1), :]
            src = xt[:].rearrange("p g u c -> p g c u")
            if j % 2 == 1:
                nc.vector.tensor_copy(out=dst, in_=src)
            else:
                nc.scalar.copy(out=dst, in_=src)
            if j % 2 == 1:
                for g in range(NPASS):
                    nc.vector.quantize_mx(
                        out=xq[:, g, P * (j - 1) : P * (j + 1)].bitcast(FP8X4),
                        scales=xs[:, g, P * (j - 1) : P * (j + 1)],
                        in_=grouped[:, g, 4 * P * (j - 1) : 4 * P * (j + 1)],
                    )

        vT = pst.tile([P, P], BF16, name="vT", tag="gT0")
        nc.tensor.transpose(vT[:], vin[:], ident_bf[:])
        bw2 = keep.tile([P, NG, 2], F32, name="bw2")
        nc.vector.tensor_copy(out=bw2[:, :, 0], in_=vT[:, 0:32])
        nc.vector.tensor_scalar(out=bw2[:, :, 1], in0=vT[:, 0:32], scalar1=-1.0, scalar2=None, op0=ALU.mult)
        bnb = keep.tile([P, NG], F32, name="bnb")
        nc.vector.tensor_copy(out=bnb[:], in_=vT[:, 32:64])
        rw = keep.tile([P, NG, NW], BF16, name="rw")
        nc.gpsimd.memset(rw[:], 0.0)
        nc.vector.memset(rw[:, :, 0], 1.0)
        nc.vector.tensor_copy(out=rw[:, :, 1], in_=vT[:, 64:96])
        rw32 = keep.tile([P, NG, NW], F32, name="rw32")
        nc.gpsimd.memset(rw32[:], 0.0)
        nc.vector.memset(rw32[:, :, 0], 1.0)
        nc.vector.tensor_copy(out=rw32[:, :, 1], in_=vT[:, 64:96])
        gwgb = keep.tile([P, 64], BF16, name="gwgb")
        nc.vector.tensor_copy(out=gwgb[:], in_=vT[:, 64:128])
        gsum_ps = pst.tile([P, 64], F32, name="gsum_ps", tag="gT1")
        nc.tensor.matmul(gsum_ps[:], lhsT=ones_bf[:], rhs=gwgb[:], start=True, stop=True)
        gsum = keep.tile([P, 64], F32, name="gsum")
        nc.vector.tensor_copy(out=gsum[:], in_=gsum_ps[:])
        gbt = keep.tile([P, 1], F32, name="gbt")
        nc.vector.tensor_reduce(out=gbt[:], in_=gsum[:, 32:64], axis=AX.X, op=ALU.add)
        gbs = keep.tile([P, 1], F32, name="gbs")
        nc.vector.tensor_scalar(out=gbs[:], in0=gbt[:], scalar1=1.0 / N, scalar2=None, op0=ALU.mult)

        s_ps = pss.tile([P, 512], F32, name="s_ps")
        st2 = keep.tile([P, NG, NJ, 6], F32, name="st2")
        ys = {}
        acts = {}
        stats = {}
        gts = {}
        late = {}
        parts = {}

        def stage_mx(G):
            y = []
            for hf in range(2):
                y.append(psy.tile([P, 512], F32, name="y%d" % hf, tag="y"))
            for hf in range(2):
                for g in range(NPASS):
                    nc.tensor.matmul_mx(
                        out=y[hf][:],
                        lhsT=wq[:, g, 256 * G : 256 * (G + 1)].bitcast(FP4X4),
                        lhsT_scale=ws[:, g, P * G : P * (G + 1)],
                        rhs=xq[:, g, 512 * hf : 512 * (hf + 1)].bitcast(FP8X4),
                        rhs_scale=xs[:, g, 512 * hf : 512 * (hf + 1)],
                        start=(g == 0),
                        stop=(g == NPASS - 1),
                    )
            ys[G] = y

        def stage_stats(G):
            y = ys[G]
            st = small.tile([P, 2, 6], F32, name="st")
            for hf in range(2):
                nc.vector.bn_stats(out=st[:, hf, :], in_=y[hf][:])
            stats[G] = st

        def stage_aggr(G):
            mv = small.tile([P, 2], F32, name="mv")
            nc.vector.bn_aggr(out=mv[:], in_=stats[G][:].rearrange("p a b -> p (a b)"))
            stats[G] = mv

        def stage_eps(G):
            mv = stats[G]
            ve = small.tile([P, 1], F32, name="ve")
            nc.vector.tensor_scalar(out=ve[:], in0=mv[:, 1:2], scalar1=EPS, scalar2=None, op0=ALU.add)
            mb = small.tile([P, 1], F32, name="mb")
            nc.vector.tensor_tensor(out=mb[:], in0=mv[:, 0:1], in1=bw2[:, G, 1:2], op=ALU.mult)
            stats[G] = (ve, mb)

        def stage_pow(G):
            ve, mb = stats[G]
            rstd = small.tile([P, 1], F32, name="rstd")
            nc.gpsimd.tensor_tensor(out=rstd[:], in0=ve[:], in1=mhalf[:], op=ALU.pow)
            stats[G] = (rstd, mb)

        def stage_gelu(G):
            y = ys[G]
            rstd, mb = stats[G]
            aa = small.tile([P, 1], F32, name="aa")
            nc.scalar.activation(out=aa[:], in_=bw2[:, G, 0:1], func=ACTF.Copy, scale=rstd[:, 0:1])
            cc = small.tile([P, 1], F32, name="cc")
            nc.scalar.activation(
                out=cc[:], in_=mb[:], func=ACTF.Identity, bias=bnb[:, G : G + 1], scale=rstd[:, 0:1]
            )
            g32 = work.tile([P, B], F32, name="g32")
            for hf in range(2):
                cols = slice(512 * hf, 512 * (hf + 1))
                nc.scalar.activation(
                    out=g32[:, cols], in_=y[hf][:], func=ACTF.Gelu, bias=cc[:, 0:1], scale=aa[:, 0:1]
                )
            acts[G] = g32

        def stage_hi_act(G):
            if G == NG - 1:
                return
            hia = work.tile([P, P * KA], BF16, name="hia")
            nc.scalar.copy(out=hia[:], in_=acts[G][:, 0 : P * KA])
            loa = work.tile([P, P * KA], BF16, name="loa")
            parts[G] = (hia, loa)

        def stage_lo_pool(G, i):
            if G == NG - 1:
                return
            hia, loa = parts[G]
            half = P * KA // 2
            cols = slice(half * i, half * (i + 1))
            nc.gpsimd.tensor_tensor(out=loa[:, cols], in0=acts[G][:, cols], in1=hia[:, cols], op=ALU.subtract)

        def stage_transpose(G, hf):
            g32 = acts[G]
            gT = pst.tile([P, 4, P], F32, name="gT%d" % hf)
            for q in range(4):
                j = 4 * hf + q
                nc.tensor.transpose(gT[:, q, :], g32[:, P * j : P * (j + 1)], ident[:])
            gts[(G, hf)] = gT

        def stage_square(G, hf, q0, q1):
            gT = gts[(G, hf)]
            for q in range(q0, q1):
                nc.vector.bn_stats(out=st2[:, G, 4 * hf + q, :], in_=gT[:, q, :])

        def stage_sums(G):
            g32 = acts[G]
            if G == LATE:
                late[0] = psy.tile([P, 512], F32, name="s_late", tag="y")
            for j in range(NJ):
                cols = slice(P * j, P * (j + 1))
                if G < LATE:
                    first = 2 * (NJ * G + j)
                    dst = s_ps[:, first : first + NW]
                else:
                    first = 2 * (NJ * (G - LATE) + j)
                    dst = late[0][:, first : first + NW]
                if j < KA and G < NG - 1:
                    hi, lo = parts[G]
                    nc.tensor.matmul(dst, lhsT=hi[:, cols], rhs=rw[:, G, :], start=True, stop=False)
                    nc.tensor.matmul(dst, lhsT=lo[:, cols], rhs=rw[:, G, :], start=False, stop=True)
                else:
                    nc.tensor.matmul(dst, lhsT=g32[:, cols], rhs=rw32[:, G, :], start=True, stop=True)

        con = keep.tile([P, NJ, NL + 1], F32, name="con")
        fin = {}

        def finish_numerator(key, sums, g0, n_g):
            shp = [P, n_g, NJ]
            sv = sums[:, 0 : 2 * NJ * n_g].rearrange("p (g j c) -> p g j c", j=NJ, c=2)
            mean = keep.tile(shp, F32, name="mean" + key)
            nc.vector.tensor_scalar(out=mean[:], in0=sv[:, :, :, 0], scalar1=1.0 / P, scalar2=None, op0=ALU.mult)
            mg = keep.tile(shp, F32, name="mg" + key)
            nc.vector.tensor_tensor(
                out=mg[:], in0=mean[:], in1=gsum[:, g0 : g0 + n_g].unsqueeze(2).to_broadcast(shp), op=ALU.mult
            )
            num = keep.tile(shp, F32, name="num" + key)
            nc.vector.tensor_tensor(out=num[:], in0=sv[:, :, :, 1], in1=mg[:], op=ALU.subtract)
            fin["mean" + key] = mean
            fin["num" + key] = num

        def variance_from_stats(key, st, dst, shp):
            dd = keep.tile(shp, F32, name="dd" + key)
            nc.vector.tensor_tensor(out=dd[:], in0=st[:, :, :, 1], in1=st[:, :, :, 4], op=ALU.subtract)
            m2 = keep.tile(shp, F32, name="m2" + key)
            nc.vector.tensor_tensor(out=m2[:], in0=st[:, :, :, 2], in1=st[:, :, :, 5], op=ALU.add)
            dq = keep.tile(shp, F32, name="dq" + key)
            nc.vector.scalar_tensor_tensor(out=dq[:], in0=dd[:], scalar=0.25, in1=dd[:], op0=ALU.mult, op1=ALU.mult)
            nc.vector.tensor_scalar(out=m2[:], in0=m2[:], scalar1=1.0 / P, scalar2=EPS, op0=ALU.mult, op1=ALU.add)
            nc.vector.tensor_tensor(out=dst, in0=m2[:], in1=dq[:], op=ALU.add)

        def finish_early_a():
            finish_numerator("e", s_ps, 0, LATE)
            var = keep.tile([P, LATE, NJ], F32, name="var_e")
            variance_from_stats("e", st2[:, 0:LATE, :, :], var[:], [P, LATE, NJ])
            fin["vare"] = var

        def finish_sqrt(key, shp):
            sd = keep.tile(shp, F32, name="sd" + key)
            nc.scalar.activation(out=sd[:], in_=fin["var" + key][:], func=ACTF.Sqrt)
            fin["sd" + key] = sd

        def finish_early_b():
            rinv = keep.tile([P, LATE, NJ], F32, name="rinv_e")
            nc.vector.reciprocal(out=rinv[:], in_=fin["sde"][:])
            num = fin["nume"]
            nc.vector.tensor_tensor(out=num[:], in0=num[:], in1=rinv[:], op=ALU.mult)
            nc.vector.tensor_reduce(out=con[:, :, NL], in_=num[:].rearrange("p g j -> p j g"), axis=AX.X, op=ALU.add)

        def finish_late_a():
            var = keep.tile([P, NL, NJ], F32, name="var_l")
            variance_from_stats("l", st2[:, LATE:NG, :, :], var[:], [P, NL, NJ])
            fin["varl"] = var

        def finish_late_b():
            rinv = keep.tile([P, NL, NJ], F32, name="rinv_l")
            nc.vector.reciprocal(out=rinv[:], in_=fin["sdl"][:])
            nc.vector.tensor_tensor(
                out=con[:, :, 0:NL].rearrange("p j g -> p g j"), in0=fin["numl"][:], in1=rinv[:], op=ALU.mult
            )
            tot = keep.tile([P, NJ], F32, name="tot")
            nc.vector.tensor_reduce(out=tot[:], in_=con[:], axis=AX.X, op=ALU.add)
            res = keep.tile([P, NJ], F32, name="res")
            nc.scalar.activation(out=res[:], in_=tot[:], func=ACTF.Relu, bias=gbs[:, 0:1], scale=1.0 / N)
            nc.sync.dma_start(out=out.rearrange("(p j) o -> p (j o)", j=NJ), in_=res[:])

        def live(G):
            return 0 <= G < NG

        with tc.manual_schedule():
            for T in range(NG + 5):
                if live(T - 4):
                    stage_square(T - 4, 1, 0, 4)
                if live(T - 2):
                    stage_hi_act(T - 2)
                if live(T - 3):
                    stage_lo_pool(T - 3, 0)
                    stage_lo_pool(T - 3, 1)
                if live(T):
                    stage_mx(T)
                if live(T - 3):
                    stage_transpose(T - 3, 0)
                    stage_transpose(T - 3, 1)
                if live(T - 4):
                    stage_sums(T - 4)
                if live(T):
                    stage_stats(T)
                    stage_aggr(T)
                if live(T - 3):
                    stage_square(T - 3, 0, 0, 2)
                if live(T):
                    stage_eps(T)
                    stage_pow(T)
                if live(T - 3):
                    stage_square(T - 3, 0, 2, 4)
                if T == NG:
                    finish_early_a()
                if live(T - 1):
                    stage_gelu(T - 1)
                if T == NG:
                    finish_sqrt("e", [P, LATE, NJ])
            finish_late_a()
            finish_sqrt("l", [P, NL, NJ])
            finish_early_b()
            finish_numerator("l", late[0], LATE, NL)
            finish_late_b()
